import numpy as np
import ml_dtypes

BF16 = ml_dtypes.bfloat16


def bf(x):
    return np.asarray(x, np.float32).astype(BF16)


def f32(x):
    return np.asarray(x, np.float32)


def f64(x):
    return np.asarray(x).astype(np.float64)


def striped(idx):
    return np.tile(idx.reshape(-1, 16).T, (8, 1))


S, H, M1, M2, N, PARTS = 1024, 128, 512, 2048, 2048, 3


def elu(v):
    return np.maximum(v, 0.0) + np.exp(np.minimum(v, 0.0)) - 1.0


def setup_inputs():
    return {
        "table": bf(np.random.standard_normal((S, H))),
        "u": bf(np.random.standard_normal((H, N))),
        "glob": bf(np.random.standard_normal((H, 1))),
        "w_task": bf(np.random.standard_normal((H, M1)) / np.sqrt(PARTS * H)),
        "w_usv": bf(np.random.standard_normal((H, M1)) / np.sqrt(PARTS * H)),
        "w_glob": bf(np.random.standard_normal((H, M1)) / np.sqrt(PARTS * H)),
        "b1": f32(0.1 * np.random.standard_normal((M1, 1))),
        "w2": bf(np.random.standard_normal((M1, M2)) / np.sqrt(M1)),
        "b2": f32(0.1 * np.random.standard_normal((M2, 1))),
        "offs": striped(np.random.permutation(np.tile(np.arange(S), 2))[:N]),
    }


def reference(table, u, glob, w_task, w_usv, w_glob, b1, w2, b2, offs):
    idx = offs[:16].T.reshape(-1)
    glob_all = np.repeat(f64(glob), N, axis=1)
    z1 = f64(w_task).T @ f64(table)[idx].T + f64(w_usv).T @ f64(u) + f64(w_glob).T @ glob_all + f64(b1)
    h1 = elu(z1)
    return elu(f64(w2).T @ h1 + f64(b2))

@@ -1,0 +1,111 @@
+import concourse.mybir as mybir
+from concourse.masks import make_identity
+
+BF16, F32, U16 = mybir.dt.bfloat16, mybir.dt.float32, mybir.dt.uint16
+ALU = mybir.AluOpType
+EXP = mybir.ActivationFunctionType.Exp
+
+P = 128
+S, H, M1, M2, N = 1024, 128, 512, 2048, 2048
+PIECE = 512
+N_PIECES = N // PIECE
+S_BLOCKS, M1_BLOCKS, M2_BLOCKS = S // P, M1 // P, M2 // P
+W2_CHUNK = 4
+
+FLOPS = 2 * N * (2 * H * M1 + M1 * M2) + 2 * H * M1
+
+
+def tile_actorcritic_b_kernel(tc, table, u, glob, w_task, w_usv, w_glob, b1, w2, b2, offs, out):
+    nc = tc.nc
+    with (
+        tc.tile_pool(name="held", bufs=1) as held,
+        tc.tile_pool(name="hidden_pool", bufs=2) as hidden_pool,
+        tc.tile_pool(name="work", bufs=3) as work,
+        tc.tile_pool(name="results", bufs=6) as results,
+        tc.psum_pool(name="banks", bufs=8) as banks,
+    ):
+        offsets = held.tile([P, N // 16], U16, name="offsets")
+        nc.sync.dma_start(offsets[:], offs)
+        rows = held.tile([P, S_BLOCKS, H], BF16, name="rows")
+        nc.sync.dma_start(rows[:], table.rearrange("(b p) h -> p b h", p=P))
+        w_task_sb = held.tile([H, M1], BF16, name="w_task_sb")
+        nc.sync.dma_start(w_task_sb[:], w_task)
+
+        w_usv_sb = held.tile([H, M1], BF16, name="w_usv_sb")
+        nc.scalar.dma_start(w_usv_sb[:], w_usv)
+        u_pieces = [held.tile([H, PIECE], BF16, name="u_piece%d" % j) for j in range(N_PIECES)]
+        nc.scalar.dma_start(u_pieces[0][:], u[:, 0:PIECE])
+        w_glob_sb = held.tile([H, M1], BF16, name="w_glob_sb")
+        nc.scalar.dma_start(w_glob_sb[:], w_glob)
+        glob_sb = held.tile([H, 1], BF16, name="glob_sb")
+        nc.scalar.dma_start(glob_sb[:], glob)
+        b1_sb = held.tile([P, M1_BLOCKS], F32, name="b1_sb")
+        b2_sb = held.tile([P, M2_BLOCKS], F32, name="b2_sb")
+        with nc.allow_non_contiguous_dma(reason="one float32 to a partition and block"):
+            nc.scalar.dma_start(b1_sb[:], b1.rearrange("(a p) o -> p (a o)", p=P))
+            nc.scalar.dma_start(b2_sb[:], b2.rearrange("(a p) o -> p (a o)", p=P))
+
+        w2_chunks = [
+            held.tile([P, M1_BLOCKS, W2_CHUNK * P], BF16, name="w2_chunk%d" % c)
+            for c in range(M2_BLOCKS // W2_CHUNK)
+        ]
+        for c, chunk in enumerate(w2_chunks):
+            columns = w2[:, c * W2_CHUNK * P : (c + 1) * W2_CHUNK * P]
+            nc.sync.dma_start(chunk[:], columns.rearrange("(k p) r -> p k r", p=P))
+        for j in range(1, N_PIECES):
+            nc.scalar.dma_start(u_pieces[j][:], u[:, j * PIECE : (j + 1) * PIECE])
+
+        identity = held.tile([P, P], BF16, name="identity")
+        make_identity(nc, identity[:])
+        window = held.tile([H, S], BF16, name="window")
+        half = S_BLOCKS // 2
+        for first in range(0, S_BLOCKS, half):
+            flipped = banks.tile([H, half * P], BF16, name="flipped", tag="bank")
+            for b in range(half):
+                nc.tensor.transpose(flipped[:, b * P : (b + 1) * P], rows[:, first + b, :], identity[:])
+            nc.vector.tensor_copy(window[:, first * P : (first + half) * P], flipped[:])
+
+        glob_part = banks.tile([P, M1_BLOCKS], F32, name="glob_part", tag="bank")
+        for a in range(M1_BLOCKS):
+            nc.tensor.matmul(glob_part[:, a : a + 1], w_glob_sb[:, a * P : (a + 1) * P], glob_sb[:], start=True, stop=True)
+        bias1 = held.tile([P, M1_BLOCKS], F32, name="bias1")
+        nc.vector.tensor_tensor(bias1[:], glob_part[:], b1_sb[:], ALU.add)
+
+        def elu_of_bank(result, bank, bias):
+            grown = work.tile([P, PIECE], F32, name="grown")
+            nc.scalar.activation(grown[:], bank[:], EXP, bias=bias)
+            below = work.tile([P, PIECE], F32, name="below")
+            nc.gpsimd.tensor_scalar(below[:], grown[:], 1.0, -1.0, ALU.min, ALU.add)
+            nc.vector.scalar_tensor_tensor(result, bank[:], bias, below[:], ALU.add, ALU.max)
+
+        def layer1(j):
+            sums = [banks.tile([P, PIECE], F32, name="sum1_%d" % a, tag="bank") for a in range(M1_BLOCKS)]
+            for a in range(M1_BLOCKS):
+                nc.tensor.matmul(sums[a][:], w_usv_sb[:, a * P : (a + 1) * P], u_pieces[j][:], start=True, stop=False)
+            looked_up = window[:].indirect(offsets[:, j * (PIECE // 16) : (j + 1) * (PIECE // 16)])
+            for a in range(M1_BLOCKS):
+                nc.tensor.matmul(sums[a][:], w_task_sb[:, a * P : (a + 1) * P], looked_up, start=False, stop=True)
+            hidden = hidden_pool.tile([P, M1_BLOCKS, PIECE], BF16, name="hidden")
+            for a in range(M1_BLOCKS):
+                elu_of_bank(hidden[:, a, :], sums[a], bias1[:, a : a + 1])
+            return hidden
+
+        def layer2(j, r, hidden):
+            chunk, q = w2_chunks[r // W2_CHUNK], r % W2_CHUNK
+            sum2 = banks.tile([P, PIECE], F32, name="sum2", tag="bank")
+            for k in range(M1_BLOCKS):
+                nc.tensor.matmul(
+                    sum2[:], chunk[:, k, q * P : (q + 1) * P], hidden[:, k, :], start=(k == 0), stop=(k == M1_BLOCKS - 1)
+                )
+            result = results.tile([P, PIECE], F32, name="result")
+            elu_of_bank(result[:], sum2, b2_sb[:, r : r + 1])
+            nc.sync.dma_start(out[r * P : (r + 1) * P, j * PIECE : (j + 1) * PIECE], result[:])
+
+        hidden = layer1(0)
+        for j in range(N_PIECES):
+            following = None
+            for r in range(M2_BLOCKS):
+                if r == M2_BLOCKS // 2 and j + 1 < N_PIECES:
+                    following = layer1(j + 1)
+                layer2(j, r, hidden)
+            hidden = following

@@ -75,7 +75,7 @@ def tile_actorcritic_b_kernel(tc, table, u, glob, w_task, w_usv, w_glob, b1, w2,
             grown = work.tile([P, PIECE], F32, name="grown")
             nc.scalar.activation(grown[:], bank[:], EXP, bias=bias)
             below = work.tile([P, PIECE], F32, name="below")
-            nc.gpsimd.tensor_scalar(below[:], grown[:], 1.0, -1.0, ALU.min, ALU.add)
+            nc.vector.tensor_scalar(below[:], grown[:], 1.0, -1.0, ALU.min, ALU.add)
             nc.vector.scalar_tensor_tensor(result, bank[:], bias, below[:], ALU.add, ALU.max)
 
         def layer1(j):

@@ -10,6 +10,7 @@ S, H, M1, M2, N = 1024, 128, 512, 2048, 2048
 PIECE = 512
 N_PIECES = N // PIECE
 S_BLOCKS, M1_BLOCKS, M2_BLOCKS = S // P, M1 // P, M2 // P
+HALF = S_BLOCKS // 2
 W2_CHUNK = 4
 
 FLOPS = 2 * N * (2 * H * M1 + M1 * M2) + 2 * H * M1
@@ -19,15 +20,16 @@ def tile_actorcritic_b_kernel(tc, table, u, glob, w_task, w_usv, w_glob, b1, w2,
     nc = tc.nc
     with (
         tc.tile_pool(name="held", bufs=1) as held,
-        tc.tile_pool(name="hidden_pool", bufs=2) as hidden_pool,
+        tc.tile_pool(name="hidden_pool", bufs=3) as hidden_pool,
         tc.tile_pool(name="work", bufs=3) as work,
         tc.tile_pool(name="results", bufs=6) as results,
         tc.psum_pool(name="banks", bufs=8) as banks,
     ):
+        rows = [held.tile([P, HALF, H], BF16, name="rows%d" % i) for i in range(2)]
+        for i, queue in enumerate((nc.sync, nc.scalar)):
+            queue.dma_start(rows[i][:], table[i * HALF * P : (i + 1) * HALF * P, :].rearrange("(b p) h -> p b h", p=P))
         offsets = held.tile([P, N // 16], U16, name="offsets")
         nc.sync.dma_start(offsets[:], offs)
-        rows = held.tile([P, S_BLOCKS, H], BF16, name="rows")
-        nc.sync.dma_start(rows[:], table.rearrange("(b p) h -> p b h", p=P))
         w_task_sb = held.tile([H, M1], BF16, name="w_task_sb")
         nc.sync.dma_start(w_task_sb[:], w_task)
 
@@ -39,6 +41,7 @@ def tile_actorcritic_b_kernel(tc, table, u, glob, w_task, w_usv, w_glob, b1, w2,
         nc.scalar.dma_start(w_glob_sb[:], w_glob)
         glob_sb = held.tile([H, 1], BF16, name="glob_sb")
         nc.scalar.dma_start(glob_sb[:], glob)
+        nc.scalar.dma_start(u_pieces[1][:], u[:, PIECE : 2 * PIECE])
         b1_sb = held.tile([P, M1_BLOCKS], F32, name="b1_sb")
         b2_sb = held.tile([P, M2_BLOCKS], F32, name="b2_sb")
         with nc.allow_non_contiguous_dma(reason="one float32 to a partition and block"):
@@ -52,24 +55,17 @@ def tile_actorcritic_b_kernel(tc, table, u, glob, w_task, w_usv, w_glob, b1, w2,
         for c, chunk in enumerate(w2_chunks):
             columns = w2[:, c * W2_CHUNK * P : (c + 1) * W2_CHUNK * P]
             nc.sync.dma_start(chunk[:], columns.rearrange("(k p) r -> p k r", p=P))
-        for j in range(1, N_PIECES):
+        for j in range(2, N_PIECES):
             nc.scalar.dma_start(u_pieces[j][:], u[:, j * PIECE : (j + 1) * PIECE])
 
         identity = held.tile([P, P], BF16, name="identity")
         make_identity(nc, identity[:])
         window = held.tile([H, S], BF16, name="window")
-        half = S_BLOCKS // 2
-        for first in range(0, S_BLOCKS, half):
-            flipped = banks.tile([H, half * P], BF16, name="flipped", tag="bank")
-            for b in range(half):
-                nc.tensor.transpose(flipped[:, b * P : (b + 1) * P], rows[:, first + b, :], identity[:])
-            nc.vector.tensor_copy(window[:, first * P : (first + half) * P], flipped[:])
-
-        glob_part = banks.tile([P, M1_BLOCKS], F32, name="glob_part", tag="bank")
-        for a in range(M1_BLOCKS):
-            nc.tensor.matmul(glob_part[:, a : a + 1], w_glob_sb[:, a * P : (a + 1) * P], glob_sb[:], start=True, stop=True)
-        bias1 = held.tile([P, M1_BLOCKS], F32, name="bias1")
-        nc.vector.tensor_tensor(bias1[:], glob_part[:], b1_sb[:], ALU.add)
+        for i in range(2):
+            flipped = banks.tile([H, HALF * P], BF16, name="flipped", tag="bank")
+            for b in range(HALF):
+                nc.tensor.transpose(flipped[:, b * P : (b + 1) * P], rows[i][:, b, :], identity[:])
+            nc.vector.tensor_copy(window[:, i * HALF * P : (i + 1) * HALF * P], flipped[:])
 
         def elu_of_bank(result, bank, bias):
             grown = work.tile([P, PIECE], F32, name="grown")
@@ -78,34 +74,57 @@ def tile_actorcritic_b_kernel(tc, table, u, glob, w_task, w_usv, w_glob, b1, w2,
             nc.vector.tensor_scalar(below[:], grown[:], 1.0, -1.0, ALU.min, ALU.add)
             nc.vector.scalar_tensor_tensor(result, bank[:], bias, below[:], ALU.add, ALU.max)
 
-        def layer1(j):
-            sums = [banks.tile([P, PIECE], F32, name="sum1_%d" % a, tag="bank") for a in range(M1_BLOCKS)]
+        sums = {}
+        hidden = {}
+
+        def take_banks(j):
             for a in range(M1_BLOCKS):
-                nc.tensor.matmul(sums[a][:], w_usv_sb[:, a * P : (a + 1) * P], u_pieces[j][:], start=True, stop=False)
+                sums[j, a] = banks.tile([P, PIECE], F32, name="sum1_%d_%d" % (j, a), tag="bank")
+
+        def add_vessels(j, opens):
+            for a in range(M1_BLOCKS):
+                nc.tensor.matmul(sums[j, a][:], w_usv_sb[:, a * P : (a + 1) * P], u_pieces[j][:], start=opens, stop=not opens)
+
+        def add_tasks(j, opens):
             looked_up = window[:].indirect(offsets[:, j * (PIECE // 16) : (j + 1) * (PIECE // 16)])
             for a in range(M1_BLOCKS):
-                nc.tensor.matmul(sums[a][:], w_task_sb[:, a * P : (a + 1) * P], looked_up, start=False, stop=True)
-            hidden = hidden_pool.tile([P, M1_BLOCKS, PIECE], BF16, name="hidden")
-            for a in range(M1_BLOCKS):
-                elu_of_bank(hidden[:, a, :], sums[a], bias1[:, a : a + 1])
-            return hidden
+                nc.tensor.matmul(sums[j, a][:], w_task_sb[:, a * P : (a + 1) * P], looked_up, start=opens, stop=not opens)
 
-        def layer2(j, r, hidden):
+        def activate(j):
+            hidden[j] = hidden_pool.tile([P, M1_BLOCKS, PIECE], BF16, name="hidden")
+            for a in range(M1_BLOCKS):
+                elu_of_bank(hidden[j][:, a, :], sums[j, a], bias1[:, a : a + 1])
+
+        def layer2(j, r):
             chunk, q = w2_chunks[r // W2_CHUNK], r % W2_CHUNK
             sum2 = banks.tile([P, PIECE], F32, name="sum2", tag="bank")
             for k in range(M1_BLOCKS):
                 nc.tensor.matmul(
-                    sum2[:], chunk[:, k, q * P : (q + 1) * P], hidden[:, k, :], start=(k == 0), stop=(k == M1_BLOCKS - 1)
+                    sum2[:], chunk[:, k, q * P : (q + 1) * P], hidden[j][:, k, :], start=(k == 0), stop=(k == M1_BLOCKS - 1)
                 )
             result = results.tile([P, PIECE], F32, name="result")
             elu_of_bank(result[:], sum2, b2_sb[:, r : r + 1])
             nc.sync.dma_start(out[r * P : (r + 1) * P, j * PIECE : (j + 1) * PIECE], result[:])
 
-        hidden = layer1(0)
+        take_banks(0)
+        add_vessels(0, opens=True)
+        glob_part = banks.tile([P, M1_BLOCKS], F32, name="glob_part", tag="bank")
+        for a in range(M1_BLOCKS):
+            nc.tensor.matmul(glob_part[:, a : a + 1], w_glob_sb[:, a * P : (a + 1) * P], glob_sb[:], start=True, stop=True)
+        bias1 = held.tile([P, M1_BLOCKS], F32, name="bias1")
+        nc.vector.tensor_tensor(bias1[:], glob_part[:], b1_sb[:], ALU.add)
+        add_tasks(0, opens=False)
+        take_banks(1)
+        add_tasks(1, opens=True)
+        add_vessels(1, opens=False)
+        activate(0)
+        activate(1)
+
         for j in range(N_PIECES):
-            following = None
             for r in range(M2_BLOCKS):
-                if r == M2_BLOCKS // 2 and j + 1 < N_PIECES:
-                    following = layer1(j + 1)
-                layer2(j, r, hidden)
-            hidden = following
+                if r == M2_BLOCKS // 2 and j + 2 < N_PIECES:
+                    take_banks(j + 2)
+                    add_vessels(j + 2, opens=True)
+                    add_tasks(j + 2, opens=False)
+                    activate(j + 2)
+                layer2(j, r)

@@ -12,6 +12,7 @@ N_PIECES = N // PIECE
 S_BLOCKS, M1_BLOCKS, M2_BLOCKS = S // P, M1 // P, M2 // P
 HALF = S_BLOCKS // 2
 W2_CHUNK = 4
+LAST_SLICE = 128
 
 FLOPS = 2 * N * (2 * H * M1 + M1 * M2) + 2 * H * M1
 
@@ -28,25 +29,23 @@ def tile_actorcritic_b_kernel(tc, table, u, glob, w_task, w_usv, w_glob, b1, w2,
         rows = [held.tile([P, HALF, H], BF16, name="rows%d" % i) for i in range(2)]
         for i, queue in enumerate((nc.sync, nc.scalar)):
             queue.dma_start(rows[i][:], table[i * HALF * P : (i + 1) * HALF * P, :].rearrange("(b p) h -> p b h", p=P))
+        w_usv_sb = held.tile([H, M1], BF16, name="w_usv_sb")
+        nc.sync.dma_start(w_usv_sb[:], w_usv)
+        u_pieces = [held.tile([H, PIECE], BF16, name="u_piece%d" % j) for j in range(N_PIECES)]
+        nc.scalar.dma_start(u_pieces[0][:], u[:, 0:PIECE])
         offsets = held.tile([P, N // 16], U16, name="offsets")
         nc.sync.dma_start(offsets[:], offs)
         w_task_sb = held.tile([H, M1], BF16, name="w_task_sb")
-        nc.sync.dma_start(w_task_sb[:], w_task)
-
-        w_usv_sb = held.tile([H, M1], BF16, name="w_usv_sb")
-        nc.scalar.dma_start(w_usv_sb[:], w_usv)
-        u_pieces = [held.tile([H, PIECE], BF16, name="u_piece%d" % j) for j in range(N_PIECES)]
-        nc.scalar.dma_start(u_pieces[0][:], u[:, 0:PIECE])
+        nc.scalar.dma_start(w_task_sb[:], w_task)
         w_glob_sb = held.tile([H, M1], BF16, name="w_glob_sb")
-        nc.scalar.dma_start(w_glob_sb[:], w_glob)
+        nc.sync.dma_start(w_glob_sb[:], w_glob)
         glob_sb = held.tile([H, 1], BF16, name="glob_sb")
         nc.scalar.dma_start(glob_sb[:], glob)
-        nc.scalar.dma_start(u_pieces[1][:], u[:, PIECE : 2 * PIECE])
         b1_sb = held.tile([P, M1_BLOCKS], F32, name="b1_sb")
         b2_sb = held.tile([P, M2_BLOCKS], F32, name="b2_sb")
         with nc.allow_non_contiguous_dma(reason="one float32 to a partition and block"):
-            nc.scalar.dma_start(b1_sb[:], b1.rearrange("(a p) o -> p (a o)", p=P))
-            nc.scalar.dma_start(b2_sb[:], b2.rearrange("(a p) o -> p (a o)", p=P))
+            nc.sync.dma_start(b1_sb[:], b1.rearrange("(a p) o -> p (a o)", p=P))
+        nc.scalar.dma_start(u_pieces[1][:], u[:, PIECE : 2 * PIECE])
 
         w2_chunks = [
             held.tile([P, M1_BLOCKS, W2_CHUNK * P], BF16, name="w2_chunk%d" % c)
@@ -55,8 +54,11 @@ def tile_actorcritic_b_kernel(tc, table, u, glob, w_task, w_usv, w_glob, b1, w2,
         for c, chunk in enumerate(w2_chunks):
             columns = w2[:, c * W2_CHUNK * P : (c + 1) * W2_CHUNK * P]
             nc.sync.dma_start(chunk[:], columns.rearrange("(k p) r -> p k r", p=P))
+            if c == 0:
+                with nc.allow_non_contiguous_dma(reason="one float32 to a partition and block"):
+                    nc.sync.dma_start(b2_sb[:], b2.rearrange("(a p) o -> p (a o)", p=P))
         for j in range(2, N_PIECES):
-            nc.scalar.dma_start(u_pieces[j][:], u[:, j * PIECE : (j + 1) * PIECE])
+            nc.sync.dma_start(u_pieces[j][:], u[:, j * PIECE : (j + 1) * PIECE])
 
         identity = held.tile([P, P], BF16, name="identity")
         make_identity(nc, identity[:])
@@ -68,9 +70,10 @@ def tile_actorcritic_b_kernel(tc, table, u, glob, w_task, w_usv, w_glob, b1, w2,
             nc.vector.tensor_copy(window[:, i * HALF * P : (i + 1) * HALF * P], flipped[:])
 
         def elu_of_bank(result, bank, bias):
-            grown = work.tile([P, PIECE], F32, name="grown")
+            width = bank.shape[-1]
+            grown = work.tile([P, width], F32, name="grown")
             nc.scalar.activation(grown[:], bank[:], EXP, bias=bias)
-            below = work.tile([P, PIECE], F32, name="below")
+            below = work.tile([P, width], F32, name="below")
             nc.vector.tensor_scalar(below[:], grown[:], 1.0, -1.0, ALU.min, ALU.add)
             nc.vector.scalar_tensor_tensor(result, bank[:], bias, below[:], ALU.add, ALU.max)
 
@@ -95,16 +98,20 @@ def tile_actorcritic_b_kernel(tc, table, u, glob, w_task, w_usv, w_glob, b1, w2,
             for a in range(M1_BLOCKS):
                 elu_of_bank(hidden[j][:, a, :], sums[j, a], bias1[:, a : a + 1])
 
-        def layer2(j, r):
+        def layer2(j, r, first=0, width=PIECE):
             chunk, q = w2_chunks[r // W2_CHUNK], r % W2_CHUNK
-            sum2 = banks.tile([P, PIECE], F32, name="sum2", tag="bank")
+            sum2 = banks.tile([P, width], F32, name="sum2", tag="bank")
             for k in range(M1_BLOCKS):
                 nc.tensor.matmul(
-                    sum2[:], chunk[:, k, q * P : (q + 1) * P], hidden[j][:, k, :], start=(k == 0), stop=(k == M1_BLOCKS - 1)
+                    sum2[:],
+                    chunk[:, k, q * P : (q + 1) * P],
+                    hidden[j][:, k, first : first + width],
+                    start=(k == 0),
+                    stop=(k == M1_BLOCKS - 1),
                 )
-            result = results.tile([P, PIECE], F32, name="result")
+            result = results.tile([P, width], F32, name="result")
             elu_of_bank(result[:], sum2, b2_sb[:, r : r + 1])
-            nc.sync.dma_start(out[r * P : (r + 1) * P, j * PIECE : (j + 1) * PIECE], result[:])
+            nc.sync.dma_start(out[r * P : (r + 1) * P, j * PIECE + first : j * PIECE + first + width], result[:])
 
         take_banks(0)
         add_vessels(0, opens=True)
@@ -127,4 +134,8 @@ def tile_actorcritic_b_kernel(tc, table, u, glob, w_task, w_usv, w_glob, b1, w2,
                     add_vessels(j + 2, opens=True)
                     add_tasks(j + 2, opens=False)
                     activate(j + 2)
-                layer2(j, r)
+                if (j, r) == (N_PIECES - 1, M2_BLOCKS - 1):
+                    for first in range(0, PIECE, LAST_SLICE):
+                        layer2(j, r, first, LAST_SLICE)
+                else:
+                    layer2(j, r)

@@ -12,7 +12,8 @@ N_PIECES = N // PIECE
 S_BLOCKS, M1_BLOCKS, M2_BLOCKS = S // P, M1 // P, M2 // P
 HALF = S_BLOCKS // 2
 W2_CHUNK = 4
-LAST_SLICE = 128
+LAST_SLICES = ((0, 256), (256, 128), (384, 128))
+VECTOR_STEP = 256
 
 FLOPS = 2 * N * (2 * H * M1 + M1 * M2) + 2 * H * M1
 
@@ -22,7 +23,7 @@ def tile_actorcritic_b_kernel(tc, table, u, glob, w_task, w_usv, w_glob, b1, w2,
     with (
         tc.tile_pool(name="held", bufs=1) as held,
         tc.tile_pool(name="hidden_pool", bufs=3) as hidden_pool,
-        tc.tile_pool(name="work", bufs=3) as work,
+        tc.tile_pool(name="work", bufs=6) as work,
         tc.tile_pool(name="results", bufs=6) as results,
         tc.psum_pool(name="banks", bufs=8) as banks,
     ):
@@ -74,8 +75,11 @@ def tile_actorcritic_b_kernel(tc, table, u, glob, w_task, w_usv, w_glob, b1, w2,
             grown = work.tile([P, width], F32, name="grown")
             nc.scalar.activation(grown[:], bank[:], EXP, bias=bias)
             below = work.tile([P, width], F32, name="below")
-            nc.vector.tensor_scalar(below[:], grown[:], 1.0, -1.0, ALU.min, ALU.add)
-            nc.vector.scalar_tensor_tensor(result, bank[:], bias, below[:], ALU.add, ALU.max)
+            parts = [slice(first, min(first + VECTOR_STEP, width)) for first in range(0, width, VECTOR_STEP)]
+            for part in parts:
+                nc.vector.tensor_scalar(below[:, part], grown[:, part], 1.0, -1.0, ALU.min, ALU.add)
+            for part in parts:
+                nc.vector.scalar_tensor_tensor(result[:, part], bank[:, part], bias, below[:, part], ALU.add, ALU.max)
 
         sums = {}
         hidden = {}
@@ -135,7 +139,7 @@ def tile_actorcritic_b_kernel(tc, table, u, glob, w_task, w_usv, w_glob, b1, w2,
                     add_tasks(j + 2, opens=False)
                     activate(j + 2)
                 if (j, r) == (N_PIECES - 1, M2_BLOCKS - 1):
-                    for first in range(0, PIECE, LAST_SLICE):
-                        layer2(j, r, first, LAST_SLICE)
+                    for first, width in LAST_SLICES:
+                        layer2(j, r, first, width)
                 else:
                     layer2(j, r)

@@ -70,15 +70,21 @@ def tile_actorcritic_b_kernel(tc, table, u, glob, w_task, w_usv, w_glob, b1, w2,
                 nc.tensor.transpose(flipped[:, b * P : (b + 1) * P], rows[i][:, b, :], identity[:])
             nc.vector.tensor_copy(window[:, i * HALF * P : (i + 1) * HALF * P], flipped[:])
 
-        def elu_of_bank(result, bank, bias):
+
+        def parts_of(width):
+            return [slice(first, min(first + VECTOR_STEP, width)) for first in range(0, width, VECTOR_STEP)]
+
+        def elu_first_step(bank, bias):
             width = bank.shape[-1]
             grown = work.tile([P, width], F32, name="grown")
             nc.scalar.activation(grown[:], bank[:], EXP, bias=bias)
             below = work.tile([P, width], F32, name="below")
-            parts = [slice(first, min(first + VECTOR_STEP, width)) for first in range(0, width, VECTOR_STEP)]
-            for part in parts:
+            for part in parts_of(width):
                 nc.vector.tensor_scalar(below[:, part], grown[:, part], 1.0, -1.0, ALU.min, ALU.add)
-            for part in parts:
+            return below
+
+        def elu_second_step(result, bank, bias, below):
+            for part in parts_of(bank.shape[-1]):
                 nc.vector.scalar_tensor_tensor(result[:, part], bank[:, part], bias, below[:, part], ALU.add, ALU.max)
 
         sums = {}
@@ -100,9 +106,10 @@ def tile_actorcritic_b_kernel(tc, table, u, glob, w_task, w_usv, w_glob, b1, w2,
         def activate(j):
             hidden[j] = hidden_pool.tile([P, M1_BLOCKS, PIECE], BF16, name="hidden")
             for a in range(M1_BLOCKS):
-                elu_of_bank(hidden[j][:, a, :], sums[j, a], bias1[:, a : a + 1])
+                below = elu_first_step(sums[j, a], bias1[:, a : a + 1])
+                elu_second_step(hidden[j][:, a, :], sums[j, a], bias1[:, a : a + 1], below)
 
-        def layer2(j, r, first=0, width=PIECE):
+        def layer2_sums(j, r, first=0, width=PIECE):
             chunk, q = w2_chunks[r // W2_CHUNK], r % W2_CHUNK
             sum2 = banks.tile([P, width], F32, name="sum2", tag="bank")
             for k in range(M1_BLOCKS):
@@ -113,8 +120,11 @@ def tile_actorcritic_b_kernel(tc, table, u, glob, w_task, w_usv, w_glob, b1, w2,
                     start=(k == 0),
                     stop=(k == M1_BLOCKS - 1),
                 )
+            return sum2, elu_first_step(sum2, b2_sb[:, r : r + 1])
+
+        def layer2_store(j, r, sum2, below, first=0, width=PIECE):
             result = results.tile([P, width], F32, name="result")
-            elu_of_bank(result[:], sum2, b2_sb[:, r : r + 1])
+            elu_second_step(result[:], sum2, b2_sb[:, r : r + 1], below)
             nc.sync.dma_start(out[r * P : (r + 1) * P, j * PIECE + first : j * PIECE + first + width], result[:])
 
         take_banks(0)
@@ -139,7 +149,9 @@ def tile_actorcritic_b_kernel(tc, table, u, glob, w_task, w_usv, w_glob, b1, w2,
                     add_tasks(j + 2, opens=False)
                     activate(j + 2)
                 if (j, r) == (N_PIECES - 1, M2_BLOCKS - 1):
-                    for first, width in LAST_SLICES:
-                        layer2(j, r, first, width)
+                    begun = [layer2_sums(j, r, first, width) for first, width in LAST_SLICES]
+                    for (sum2, below), (first, width) in zip(begun, LAST_SLICES):
+                        layer2_store(j, r, sum2, below, first, width)
                 else:
-                    layer2(j, r)
+                    sum2, below = layer2_sums(j, r)
+                    layer2_store(j, r, sum2, below)

@@ -29,7 +29,7 @@ def tile_actorcritic_b_kernel(tc, table, u, glob, w_task, w_usv, w_glob, b1, w2,
     ):
         rows = [held.tile([P, HALF, H], BF16, name="rows%d" % i) for i in range(2)]
         for i, queue in enumerate((nc.sync, nc.scalar)):
-            queue.dma_start(rows[i][:], table[i * HALF * P : (i + 1) * HALF * P, :].rearrange("(b p) h -> p b h", p=P))
+            queue.dma_start(rows[i][:], table[i * HALF * P : (i + 1) * HALF * P, :].rearrange("(p b) h -> p b h", p=P))
         w_usv_sb = held.tile([H, M1], BF16, name="w_usv_sb")
         nc.sync.dma_start(w_usv_sb[:], w_usv)
         u_pieces = [held.tile([H, PIECE], BF16, name="u_piece%d" % j) for j in range(N_PIECES)]
@@ -68,7 +68,10 @@ def tile_actorcritic_b_kernel(tc, table, u, glob, w_task, w_usv, w_glob, b1, w2,
             flipped = banks.tile([H, HALF * P], BF16, name="flipped", tag="bank")
             for b in range(HALF):
                 nc.tensor.transpose(flipped[:, b * P : (b + 1) * P], rows[i][:, b, :], identity[:])
-            nc.vector.tensor_copy(window[:, i * HALF * P : (i + 1) * HALF * P], flipped[:])
+            nc.vector.tensor_copy(
+                window[:, i * HALF * P : (i + 1) * HALF * P].rearrange("h (p b) -> h p b", p=P),
+                flipped[:].rearrange("h (b p) -> h p b", p=P),
+            )
 
 
         def parts_of(width):

@@ -23,7 +23,7 @@ def tile_actorcritic_b_kernel(tc, table, u, glob, w_task, w_usv, w_glob, b1, w2,
     with (
         tc.tile_pool(name="held", bufs=1) as held,
         tc.tile_pool(name="hidden_pool", bufs=3) as hidden_pool,
-        tc.tile_pool(name="work", bufs=6) as work,
+        tc.tile_pool(name="work", bufs=3) as work,
         tc.tile_pool(name="results", bufs=6) as results,
         tc.psum_pool(name="banks", bufs=8) as banks,
     ):

@@ -11,6 +11,7 @@ PIECE = 512
 N_PIECES = N // PIECE
 S_BLOCKS, M1_BLOCKS, M2_BLOCKS = S // P, M1 // P, M2 // P
 HALF = S_BLOCKS // 2
+FLIPS_A_MATMUL = S_BLOCKS // M1_BLOCKS
 W2_CHUNK = 4
 LAST_SLICES = ((0, 256), (256, 128), (384, 128))
 VECTOR_STEP = 256
@@ -27,26 +28,26 @@ def tile_actorcritic_b_kernel(tc, table, u, glob, w_task, w_usv, w_glob, b1, w2,
         tc.tile_pool(name="results", bufs=6) as results,
         tc.psum_pool(name="banks", bufs=8) as banks,
     ):
-        rows = [held.tile([P, HALF, H], BF16, name="rows%d" % i) for i in range(2)]
-        for i, queue in enumerate((nc.sync, nc.scalar)):
-            queue.dma_start(rows[i][:], table[i * HALF * P : (i + 1) * HALF * P, :].rearrange("(p b) h -> p b h", p=P))
         w_usv_sb = held.tile([H, M1], BF16, name="w_usv_sb")
         nc.sync.dma_start(w_usv_sb[:], w_usv)
         u_pieces = [held.tile([H, PIECE], BF16, name="u_piece%d" % j) for j in range(N_PIECES)]
         nc.scalar.dma_start(u_pieces[0][:], u[:, 0:PIECE])
-        offsets = held.tile([P, N // 16], U16, name="offsets")
-        nc.sync.dma_start(offsets[:], offs)
-        w_task_sb = held.tile([H, M1], BF16, name="w_task_sb")
-        nc.scalar.dma_start(w_task_sb[:], w_task)
+        rows = [held.tile([P, HALF, H], BF16, name="rows%d" % i) for i in range(2)]
+        for i, queue in enumerate((nc.sync, nc.scalar)):
+            queue.dma_start(rows[i][:], table[i * HALF * P : (i + 1) * HALF * P, :].rearrange("(p b) h -> p b h", p=P))
         w_glob_sb = held.tile([H, M1], BF16, name="w_glob_sb")
         nc.sync.dma_start(w_glob_sb[:], w_glob)
         glob_sb = held.tile([H, 1], BF16, name="glob_sb")
         nc.scalar.dma_start(glob_sb[:], glob)
+        offsets = held.tile([P, N // 16], U16, name="offsets")
+        nc.sync.dma_start(offsets[:], offs)
+        nc.scalar.dma_start(u_pieces[1][:], u[:, PIECE : 2 * PIECE])
         b1_sb = held.tile([P, M1_BLOCKS], F32, name="b1_sb")
         b2_sb = held.tile([P, M2_BLOCKS], F32, name="b2_sb")
         with nc.allow_non_contiguous_dma(reason="one float32 to a partition and block"):
             nc.sync.dma_start(b1_sb[:], b1.rearrange("(a p) o -> p (a o)", p=P))
-        nc.scalar.dma_start(u_pieces[1][:], u[:, PIECE : 2 * PIECE])
+        w_task_sb = held.tile([H, M1], BF16, name="w_task_sb")
+        nc.scalar.dma_start(w_task_sb[:], w_task)
 
         w2_chunks = [
             held.tile([P, M1_BLOCKS, W2_CHUNK * P], BF16, name="w2_chunk%d" % c)
@@ -64,14 +65,6 @@ def tile_actorcritic_b_kernel(tc, table, u, glob, w_task, w_usv, w_glob, b1, w2,
         identity = held.tile([P, P], BF16, name="identity")
         make_identity(nc, identity[:])
         window = held.tile([H, S], BF16, name="window")
-        for i in range(2):
-            flipped = banks.tile([H, HALF * P], BF16, name="flipped", tag="bank")
-            for b in range(HALF):
-                nc.tensor.transpose(flipped[:, b * P : (b + 1) * P], rows[i][:, b, :], identity[:])
-            nc.vector.tensor_copy(
-                window[:, i * HALF * P : (i + 1) * HALF * P].rearrange("h (p b) -> h p b", p=P),
-                flipped[:].rearrange("h (b p) -> h p b", p=P),
-            )
 
 
         def parts_of(width):
@@ -93,18 +86,14 @@ def tile_actorcritic_b_kernel(tc, table, u, glob, w_task, w_usv, w_glob, b1, w2,
         sums = {}
         hidden = {}
 
-        def take_banks(j):
-            for a in range(M1_BLOCKS):
-                sums[j, a] = banks.tile([P, PIECE], F32, name="sum1_%d_%d" % (j, a), tag="bank")
+        def add_vessels(j, a):
+            sums[j, a] = banks.tile([P, PIECE], F32, name="sum1_%d_%d" % (j, a), tag="bank")
+            nc.tensor.matmul(sums[j, a][:], w_usv_sb[:, a * P : (a + 1) * P], u_pieces[j][:], start=True, stop=False)
 
-        def add_vessels(j, opens):
-            for a in range(M1_BLOCKS):
-                nc.tensor.matmul(sums[j, a][:], w_usv_sb[:, a * P : (a + 1) * P], u_pieces[j][:], start=opens, stop=not opens)
-
-        def add_tasks(j, opens):
+        def add_tasks(j):
             looked_up = window[:].indirect(offsets[:, j * (PIECE // 16) : (j + 1) * (PIECE // 16)])
             for a in range(M1_BLOCKS):
-                nc.tensor.matmul(sums[j, a][:], w_task_sb[:, a * P : (a + 1) * P], looked_up, start=opens, stop=not opens)
+                nc.tensor.matmul(sums[j, a][:], w_task_sb[:, a * P : (a + 1) * P], looked_up, start=False, stop=True)
 
         def activate(j):
             hidden[j] = hidden_pool.tile([P, M1_BLOCKS, PIECE], BF16, name="hidden")
@@ -130,26 +119,35 @@ def tile_actorcritic_b_kernel(tc, table, u, glob, w_task, w_usv, w_glob, b1, w2,
             elu_second_step(result[:], sum2, b2_sb[:, r : r + 1], below)
             nc.sync.dma_start(out[r * P : (r + 1) * P, j * PIECE + first : j * PIECE + first + width], result[:])
 
-        take_banks(0)
-        add_vessels(0, opens=True)
+        flipped = [banks.tile([H, HALF * P], BF16, name="flipped%d" % i, tag="bank") for i in range(2)]
+        for a in range(M1_BLOCKS):
+            add_vessels(0, a)
+            for block in range(a * FLIPS_A_MATMUL, (a + 1) * FLIPS_A_MATMUL):
+                i, b = divmod(block, HALF)
+                nc.tensor.transpose(flipped[i][:, b * P : (b + 1) * P], rows[i][:, b, :], identity[:])
+            if (a + 1) * FLIPS_A_MATMUL % HALF == 0:
+                nc.vector.tensor_copy(
+                    window[:, i * HALF * P : (i + 1) * HALF * P].rearrange("h (p b) -> h p b", p=P),
+                    flipped[i][:].rearrange("h (b p) -> h p b", p=P),
+                )
         glob_part = banks.tile([P, M1_BLOCKS], F32, name="glob_part", tag="bank")
         for a in range(M1_BLOCKS):
             nc.tensor.matmul(glob_part[:, a : a + 1], w_glob_sb[:, a * P : (a + 1) * P], glob_sb[:], start=True, stop=True)
         bias1 = held.tile([P, M1_BLOCKS], F32, name="bias1")
         nc.vector.tensor_tensor(bias1[:], glob_part[:], b1_sb[:], ALU.add)
-        add_tasks(0, opens=False)
-        take_banks(1)
-        add_tasks(1, opens=True)
-        add_vessels(1, opens=False)
+        for a in range(M1_BLOCKS):
+            add_vessels(1, a)
+        add_tasks(0)
+        add_tasks(1)
         activate(0)
         activate(1)
 
         for j in range(N_PIECES):
             for r in range(M2_BLOCKS):
                 if r == M2_BLOCKS // 2 and j + 2 < N_PIECES:
-                    take_banks(j + 2)
-                    add_vessels(j + 2, opens=True)
-                    add_tasks(j + 2, opens=False)
+                    for a in range(M1_BLOCKS):
+                        add_vessels(j + 2, a)
+                    add_tasks(j + 2)
                     activate(j + 2)
                 if (j, r) == (N_PIECES - 1, M2_BLOCKS - 1):
                     begun = [layer2_sums(j, r, first, width) for first, width in LAST_SLICES]

@@ -11,7 +11,6 @@ PIECE = 512
 N_PIECES = N // PIECE
 S_BLOCKS, M1_BLOCKS, M2_BLOCKS = S // P, M1 // P, M2 // P
 HALF = S_BLOCKS // 2
-FLIPS_A_MATMUL = S_BLOCKS // M1_BLOCKS
 W2_CHUNK = 4
 LAST_SLICES = ((0, 256), (256, 128), (384, 128))
 VECTOR_STEP = 256
@@ -41,13 +40,13 @@ def tile_actorcritic_b_kernel(tc, table, u, glob, w_task, w_usv, w_glob, b1, w2,
         nc.scalar.dma_start(glob_sb[:], glob)
         offsets = held.tile([P, N // 16], U16, name="offsets")
         nc.sync.dma_start(offsets[:], offs)
-        nc.scalar.dma_start(u_pieces[1][:], u[:, PIECE : 2 * PIECE])
+        w_task_sb = held.tile([H, M1], BF16, name="w_task_sb")
+        nc.scalar.dma_start(w_task_sb[:], w_task)
         b1_sb = held.tile([P, M1_BLOCKS], F32, name="b1_sb")
         b2_sb = held.tile([P, M2_BLOCKS], F32, name="b2_sb")
         with nc.allow_non_contiguous_dma(reason="one float32 to a partition and block"):
             nc.sync.dma_start(b1_sb[:], b1.rearrange("(a p) o -> p (a o)", p=P))
-        w_task_sb = held.tile([H, M1], BF16, name="w_task_sb")
-        nc.scalar.dma_start(w_task_sb[:], w_task)
+        nc.scalar.dma_start(u_pieces[1][:], u[:, PIECE : 2 * PIECE])
 
         w2_chunks = [
             held.tile([P, M1_BLOCKS, W2_CHUNK * P], BF16, name="w2_chunk%d" % c)
@@ -65,6 +64,15 @@ def tile_actorcritic_b_kernel(tc, table, u, glob, w_task, w_usv, w_glob, b1, w2,
         identity = held.tile([P, P], BF16, name="identity")
         make_identity(nc, identity[:])
         window = held.tile([H, S], BF16, name="window")
+
+        def flip_half(i):
+            flipped = banks.tile([H, HALF * P], BF16, name="flipped", tag="bank")
+            for b in range(HALF):
+                nc.tensor.transpose(flipped[:, b * P : (b + 1) * P], rows[i][:, b, :], identity[:])
+            nc.vector.tensor_copy(
+                window[:, i * HALF * P : (i + 1) * HALF * P].rearrange("h (p b) -> h p b", p=P),
+                flipped[:].rearrange("h (b p) -> h p b", p=P),
+            )
 
 
         def parts_of(width):
@@ -86,14 +94,17 @@ def tile_actorcritic_b_kernel(tc, table, u, glob, w_task, w_usv, w_glob, b1, w2,
         sums = {}
         hidden = {}
 
-        def add_vessels(j, a):
-            sums[j, a] = banks.tile([P, PIECE], F32, name="sum1_%d_%d" % (j, a), tag="bank")
-            nc.tensor.matmul(sums[j, a][:], w_usv_sb[:, a * P : (a + 1) * P], u_pieces[j][:], start=True, stop=False)
+        def take_banks(j):
+            for a in range(M1_BLOCKS):
+                sums[j, a] = banks.tile([P, PIECE], F32, name="sum1_%d_%d" % (j, a), tag="bank")
 
-        def add_tasks(j):
+        def add_vessels(j, a, opens):
+            nc.tensor.matmul(sums[j, a][:], w_usv_sb[:, a * P : (a + 1) * P], u_pieces[j][:], start=opens, stop=not opens)
+
+        def add_tasks(j, opens):
             looked_up = window[:].indirect(offsets[:, j * (PIECE // 16) : (j + 1) * (PIECE // 16)])
             for a in range(M1_BLOCKS):
-                nc.tensor.matmul(sums[j, a][:], w_task_sb[:, a * P : (a + 1) * P], looked_up, start=False, stop=True)
+                nc.tensor.matmul(sums[j, a][:], w_task_sb[:, a * P : (a + 1) * P], looked_up, start=opens, stop=not opens)
 
         def activate(j):
             hidden[j] = hidden_pool.tile([P, M1_BLOCKS, PIECE], BF16, name="hidden")
@@ -119,35 +130,31 @@ def tile_actorcritic_b_kernel(tc, table, u, glob, w_task, w_usv, w_glob, b1, w2,
             elu_second_step(result[:], sum2, b2_sb[:, r : r + 1], below)
             nc.sync.dma_start(out[r * P : (r + 1) * P, j * PIECE + first : j * PIECE + first + width], result[:])
 
-        flipped = [banks.tile([H, HALF * P], BF16, name="flipped%d" % i, tag="bank") for i in range(2)]
+        take_banks(0)
         for a in range(M1_BLOCKS):
-            add_vessels(0, a)
-            for block in range(a * FLIPS_A_MATMUL, (a + 1) * FLIPS_A_MATMUL):
-                i, b = divmod(block, HALF)
-                nc.tensor.transpose(flipped[i][:, b * P : (b + 1) * P], rows[i][:, b, :], identity[:])
-            if (a + 1) * FLIPS_A_MATMUL % HALF == 0:
-                nc.vector.tensor_copy(
-                    window[:, i * HALF * P : (i + 1) * HALF * P].rearrange("h (p b) -> h p b", p=P),
-                    flipped[i][:].rearrange("h (b p) -> h p b", p=P),
-                )
+            add_vessels(0, a, opens=True)
+            if a < 2:
+                flip_half(a)
         glob_part = banks.tile([P, M1_BLOCKS], F32, name="glob_part", tag="bank")
         for a in range(M1_BLOCKS):
             nc.tensor.matmul(glob_part[:, a : a + 1], w_glob_sb[:, a * P : (a + 1) * P], glob_sb[:], start=True, stop=True)
         bias1 = held.tile([P, M1_BLOCKS], F32, name="bias1")
         nc.vector.tensor_tensor(bias1[:], glob_part[:], b1_sb[:], ALU.add)
+        add_tasks(0, opens=False)
+        take_banks(1)
+        add_tasks(1, opens=True)
         for a in range(M1_BLOCKS):
-            add_vessels(1, a)
-        add_tasks(0)
-        add_tasks(1)
+            add_vessels(1, a, opens=False)
         activate(0)
         activate(1)
 
         for j in range(N_PIECES):
             for r in range(M2_BLOCKS):
                 if r == M2_BLOCKS // 2 and j + 2 < N_PIECES:
+                    take_banks(j + 2)
                     for a in range(M1_BLOCKS):
-                        add_vessels(j + 2, a)
-                    add_tasks(j + 2)
+                        add_vessels(j + 2, a, opens=True)
+                    add_tasks(j + 2, opens=False)
                     activate(j + 2)
                 if (j, r) == (N_PIECES - 1, M2_BLOCKS - 1):
                     begun = [layer2_sums(j, r, first, width) for first, width in LAST_SLICES]

@@ -4,6 +4,7 @@ from concourse.masks import make_identity
 BF16, F32, U16 = mybir.dt.bfloat16, mybir.dt.float32, mybir.dt.uint16
 ALU = mybir.AluOpType
 EXP = mybir.ActivationFunctionType.Exp
+RELU = mybir.ActivationFunctionType.Relu
 
 P = 128
 S, H, M1, M2, N = 1024, 128, 512, 2048, 2048
@@ -91,6 +92,14 @@ def tile_actorcritic_b_kernel(tc, table, u, glob, w_task, w_usv, w_glob, b1, w2,
             for part in parts_of(bank.shape[-1]):
                 nc.vector.scalar_tensor_tensor(result[:, part], bank[:, part], bias, below[:, part], ALU.add, ALU.max)
 
+        def elu_short_on_vector(result, bank, bias):
+            width = bank.shape[-1]
+            grown = work.tile([P, width], F32, name="grown")
+            nc.scalar.activation(grown[:], bank[:], EXP, bias=bias)
+            kept = work.tile([P, width], F32, name="kept")
+            nc.scalar.activation(kept[:], bank[:], RELU, bias=bias)
+            nc.vector.scalar_tensor_tensor(result, grown[:], -1.0, kept[:], ALU.add, ALU.min)
+
         sums = {}
         hidden = {}
 
@@ -123,11 +132,9 @@ def tile_actorcritic_b_kernel(tc, table, u, glob, w_task, w_usv, w_glob, b1, w2,
                     start=(k == 0),
                     stop=(k == M1_BLOCKS - 1),
                 )
-            return sum2, elu_first_step(sum2, b2_sb[:, r : r + 1])
+            return sum2
 
-        def layer2_store(j, r, sum2, below, first=0, width=PIECE):
-            result = results.tile([P, width], F32, name="result")
-            elu_second_step(result[:], sum2, b2_sb[:, r : r + 1], below)
+        def store(j, r, result, first=0, width=PIECE):
             nc.sync.dma_start(out[r * P : (r + 1) * P, j * PIECE + first : j * PIECE + first + width], result[:])
 
         take_banks(0)
@@ -156,10 +163,22 @@ def tile_actorcritic_b_kernel(tc, table, u, glob, w_task, w_usv, w_glob, b1, w2,
                         add_vessels(j + 2, a, opens=True)
                     add_tasks(j + 2, opens=False)
                     activate(j + 2)
+                bias = b2_sb[:, r : r + 1]
                 if (j, r) == (N_PIECES - 1, M2_BLOCKS - 1):
-                    begun = [layer2_sums(j, r, first, width) for first, width in LAST_SLICES]
-                    for (sum2, below), (first, width) in zip(begun, LAST_SLICES):
-                        layer2_store(j, r, sum2, below, first, width)
+                    for first, width in LAST_SLICES:
+                        sum2 = layer2_sums(j, r, first, width)
+                        result = results.tile([P, width], F32, name="result")
+                        elu_short_on_vector(result[:], sum2, bias)
+                        store(j, r, result, first, width)
                 else:
-                    sum2, below = layer2_sums(j, r)
-                    layer2_store(j, r, sum2, below)
+                    sum2 = layer2_sums(j, r)
+                    below = elu_first_step(sum2, bias)
+                    result = results.tile([P, PIECE], F32, name="result")
+                    elu_second_step(result[:], sum2, bias, below)
+                    if j == N_PIECES - 1 and r >= M2_BLOCKS - 3:
+                        for part in parts_of(PIECE):
+                            nc.sync.dma_start(
+                                out[r * P : (r + 1) * P, j * PIECE + part.start : j * PIECE + part.stop], result[:, part]
+                            )
+                    else:
+                        store(j, r, result)

@@ -82,7 +82,8 @@ def tile_actorcritic_b_kernel(tc, table, u, glob, w_task, w_usv, w_glob, b1, w2,
         def elu_first_step(bank, bias):
             width = bank.shape[-1]
             grown = work.tile([P, width], F32, name="grown")
-            nc.scalar.activation(grown[:], bank[:], EXP, bias=bias)
+            for part in parts_of(width):
+                nc.scalar.activation(grown[:, part], bank[:, part], EXP, bias=bias)
             below = work.tile([P, width], F32, name="below")
             for part in parts_of(width):
                 nc.vector.tensor_scalar(below[:, part], grown[:, part], 1.0, -1.0, ALU.min, ALU.add)

import concourse.mybir as mybir
from concourse.masks import make_identity

BF16, F32, U16 = mybir.dt.bfloat16, mybir.dt.float32, mybir.dt.uint16
ALU = mybir.AluOpType
EXP = mybir.ActivationFunctionType.Exp
RELU = mybir.ActivationFunctionType.Relu

P = 128
S, H, M1, M2, N = 1024, 128, 512, 2048, 2048
PIECE = 512
N_PIECES = N // PIECE
S_BLOCKS, M1_BLOCKS, M2_BLOCKS = S // P, M1 // P, M2 // P
HALF = S_BLOCKS // 2
W2_CHUNK = 4
LAST_SLICES = ((0, 256), (256, 128), (384, 128))
VECTOR_STEP = 256

FLOPS = 2 * N * (2 * H * M1 + M1 * M2) + 2 * H * M1


def tile_actorcritic_b_kernel(tc, table, u, glob, w_task, w_usv, w_glob, b1, w2, b2, offs, out):
    nc = tc.nc
    with (
        tc.tile_pool(name="held", bufs=1) as held,
        tc.tile_pool(name="hidden_pool", bufs=3) as hidden_pool,
        tc.tile_pool(name="work", bufs=3) as work,
        tc.tile_pool(name="results", bufs=6) as results,
        tc.psum_pool(name="banks", bufs=8) as banks,
    ):
        w_usv_sb = held.tile([H, M1], BF16, name="w_usv_sb")
        nc.sync.dma_start(w_usv_sb[:], w_usv)
        u_pieces = [held.tile([H, PIECE], BF16, name="u_piece%d" % j) for j in range(N_PIECES)]
        nc.scalar.dma_start(u_pieces[0][:], u[:, 0:PIECE])
        rows = [held.tile([P, HALF, H], BF16, name="rows%d" % i) for i in range(2)]
        for i, queue in enumerate((nc.sync, nc.scalar)):
            queue.dma_start(rows[i][:], table[i * HALF * P : (i + 1) * HALF * P, :].rearrange("(p b) h -> p b h", p=P))
        w_glob_sb = held.tile([H, M1], BF16, name="w_glob_sb")
        nc.sync.dma_start(w_glob_sb[:], w_glob)
        glob_sb = held.tile([H, 1], BF16, name="glob_sb")
        nc.scalar.dma_start(glob_sb[:], glob)
        offsets = held.tile([P, N // 16], U16, name="offsets")
        nc.sync.dma_start(offsets[:], offs)
        w_task_sb = held.tile([H, M1], BF16, name="w_task_sb")
        nc.scalar.dma_start(w_task_sb[:], w_task)
        b1_sb = held.tile([P, M1_BLOCKS], F32, name="b1_sb")
        b2_sb = held.tile([P, M2_BLOCKS], F32, name="b2_sb")
        with nc.allow_non_contiguous_dma(reason="one float32 to a partition and block"):
            nc.sync.dma_start(b1_sb[:], b1.rearrange("(a p) o -> p (a o)", p=P))
        nc.scalar.dma_start(u_pieces[1][:], u[:, PIECE : 2 * PIECE])

        w2_chunks = [
            held.tile([P, M1_BLOCKS, W2_CHUNK * P], BF16, name="w2_chunk%d" % c)
            for c in range(M2_BLOCKS // W2_CHUNK)
        ]
        for c, chunk in enumerate(w2_chunks):
            columns = w2[:, c * W2_CHUNK * P : (c + 1) * W2_CHUNK * P]
            nc.sync.dma_start(chunk[:], columns.rearrange("(k p) r -> p k r", p=P))
            if c == 0:
                with nc.allow_non_contiguous_dma(reason="one float32 to a partition and block"):
                    nc.sync.dma_start(b2_sb[:], b2.rearrange("(a p) o -> p (a o)", p=P))
        for j in range(2, N_PIECES):
            nc.sync.dma_start(u_pieces[j][:], u[:, j * PIECE : (j + 1) * PIECE])

        identity = held.tile([P, P], BF16, name="identity")
        make_identity(nc, identity[:])
        window = held.tile([H, S], BF16, name="window")

        def flip_half(i):
            flipped = banks.tile([H, HALF * P], BF16, name="flipped", tag="bank")
            for b in range(HALF):
                nc.tensor.transpose(flipped[:, b * P : (b + 1) * P], rows[i][:, b, :], identity[:])
            nc.vector.tensor_copy(
                window[:, i * HALF * P : (i + 1) * HALF * P].rearrange("h (p b) -> h p b", p=P),
                flipped[:].rearrange("h (b p) -> h p b", p=P),
            )


        def parts_of(width):
            return [slice(first, min(first + VECTOR_STEP, width)) for first in range(0, width, VECTOR_STEP)]

        def elu_first_step(bank, bias):
            width = bank.shape[-1]
            grown = work.tile([P, width], F32, name="grown")
            for part in parts_of(width):
                nc.scalar.activation(grown[:, part], bank[:, part], EXP, bias=bias)
            below = work.tile([P, width], F32, name="below")
            for part in parts_of(width):
                nc.vector.tensor_scalar(below[:, part], grown[:, part], 1.0, -1.0, ALU.min, ALU.add)
            return below

        def elu_second_step(result, bank, bias, below):
            for part in parts_of(bank.shape[-1]):
                nc.vector.scalar_tensor_tensor(result[:, part], bank[:, part], bias, below[:, part], ALU.add, ALU.max)

        def elu_short_on_vector(result, bank, bias):
            width = bank.shape[-1]
            grown = work.tile([P, width], F32, name="grown")
            nc.scalar.activation(grown[:], bank[:], EXP, bias=bias)
            kept = work.tile([P, width], F32, name="kept")
            nc.scalar.activation(kept[:], bank[:], RELU, bias=bias)
            nc.vector.scalar_tensor_tensor(result, grown[:], -1.0, kept[:], ALU.add, ALU.min)

        sums = {}
        hidden = {}

        def take_banks(j):
            for a in range(M1_BLOCKS):
                sums[j, a] = banks.tile([P, PIECE], F32, name="sum1_%d_%d" % (j, a), tag="bank")

        def add_vessels(j, a, opens):
            nc.tensor.matmul(sums[j, a][:], w_usv_sb[:, a * P : (a + 1) * P], u_pieces[j][:], start=opens, stop=not opens)

        def add_tasks(j, opens):
            looked_up = window[:].indirect(offsets[:, j * (PIECE // 16) : (j + 1) * (PIECE // 16)])
            for a in range(M1_BLOCKS):
                nc.tensor.matmul(sums[j, a][:], w_task_sb[:, a * P : (a + 1) * P], looked_up, start=opens, stop=not opens)

        def activate(j):
            hidden[j] = hidden_pool.tile([P, M1_BLOCKS, PIECE], BF16, name="hidden")
            for a in range(M1_BLOCKS):
                below = elu_first_step(sums[j, a], bias1[:, a : a + 1])
                elu_second_step(hidden[j][:, a, :], sums[j, a], bias1[:, a : a + 1], below)

        def layer2_sums(j, r, first=0, width=PIECE):
            chunk, q = w2_chunks[r // W2_CHUNK], r % W2_CHUNK
            sum2 = banks.tile([P, width], F32, name="sum2", tag="bank")
            for k in range(M1_BLOCKS):
                nc.tensor.matmul(
                    sum2[:],
                    chunk[:, k, q * P : (q + 1) * P],
                    hidden[j][:, k, first : first + width],
                    start=(k == 0),
                    stop=(k == M1_BLOCKS - 1),
                )
            return sum2

        def store(j, r, result, first=0, width=PIECE):
            nc.sync.dma_start(out[r * P : (r + 1) * P, j * PIECE + first : j * PIECE + first + width], result[:])

        take_banks(0)
        for a in range(M1_BLOCKS):
            add_vessels(0, a, opens=True)
            if a < 2:
                flip_half(a)
        glob_part = banks.tile([P, M1_BLOCKS], F32, name="glob_part", tag="bank")
        for a in range(M1_BLOCKS):
            nc.tensor.matmul(glob_part[:, a : a + 1], w_glob_sb[:, a * P : (a + 1) * P], glob_sb[:], start=True, stop=True)
        bias1 = held.tile([P, M1_BLOCKS], F32, name="bias1")
        nc.vector.tensor_tensor(bias1[:], glob_part[:], b1_sb[:], ALU.add)
        add_tasks(0, opens=False)
        take_banks(1)
        add_tasks(1, opens=True)
        for a in range(M1_BLOCKS):
            add_vessels(1, a, opens=False)
        activate(0)
        activate(1)

        for j in range(N_PIECES):
            for r in range(M2_BLOCKS):
                if r == M2_BLOCKS // 2 and j + 2 < N_PIECES:
                    take_banks(j + 2)
                    for a in range(M1_BLOCKS):
                        add_vessels(j + 2, a, opens=True)
                    add_tasks(j + 2, opens=False)
                    activate(j + 2)
                bias = b2_sb[:, r : r + 1]
                if (j, r) == (N_PIECES - 1, M2_BLOCKS - 1):
                    for first, width in LAST_SLICES:
                        sum2 = layer2_sums(j, r, first, width)
                        result = results.tile([P, width], F32, name="result")
                        elu_short_on_vector(result[:], sum2, bias)
                        store(j, r, result, first, width)
                else:
                    sum2 = layer2_sums(j, r)
                    below = elu_first_step(sum2, bias)
                    result = results.tile([P, PIECE], F32, name="result")
                    elu_second_step(result[:], sum2, bias, below)
                    if j == N_PIECES - 1 and r >= M2_BLOCKS - 3:
                        for part in parts_of(PIECE):
                            nc.sync.dma_start(
                                out[r * P : (r + 1) * P, j * PIECE + part.start : j * PIECE + part.stop], result[:, part]
                            )
                    else:
                        store(j, r, result)
